import numpy as np
import ml_dtypes

BF16 = ml_dtypes.bfloat16


def bf(x):
    return np.asarray(x, np.float32).astype(BF16)


def f32(x):
    return np.asarray(x, np.float32)


def f64(x):
    return np.asarray(x).astype(np.float64)


def striped(idx):
    return np.tile(idx.reshape(-1, 16).T, (8, 1))


D, S, H, N, L = 128, 4096, 512, 1024, 3


def sigmoid(v):
    return 1.0 / (1.0 + np.exp(-v))


def setup_inputs():
    w = lambda: bf(np.random.standard_normal((D, H)) / np.sqrt(D))
    u = lambda: bf(2.0 * np.random.standard_normal((H, H)) / np.sqrt(H))
    b = lambda: f32(0.5 * np.random.standard_normal((H, 1)))
    return {"table": bf(np.random.standard_normal((D, S))), "w_z_l": w(), "w_z_r": w(), "w_h_l": w(), "w_h_r": w(), "u_z_l": u(), "u_z_r": u(), "u_h_l": u(), "u_h_r": u(), "b_z": b(), "b_h": b(), "offs": striped(np.random.permutation(np.tile(np.arange(S), 2))[:N])}


def reference(table, w_z_l, w_z_r, w_h_l, w_h_r, u_z_l, u_z_r, u_h_l, u_h_r, b_z, b_h, offs):
    idx = offs[:16].T.reshape(-1)
    e = f64(table)[:, idx]
    n = N // 2
    e_l, e_r = e[:, :n], e[:, n:]
    z = sigmoid(f64(w_z_l).T @ e_l + f64(w_z_r).T @ e_r + f64(b_z))
    t = sigmoid(f64(w_h_l).T @ e_l + f64(w_h_r).T @ e_r + f64(b_h))
    h = (1.0 - z) * t
    for _ in range(L - 1):
        n = n // 2
        h_l, h_r = h[:, :n], h[:, n:]
        z = sigmoid(f64(u_z_l).T @ h_l + f64(u_z_r).T @ h_r + f64(b_z))
        t = sigmoid(f64(u_h_l).T @ h_l + f64(u_h_r).T @ h_r + f64(b_h))
        h = z * (h_l + h_r) + (1.0 - z) * t
    return h

@@ -1,0 +1,138 @@
+import concourse.mybir as mybir
+
+BF16, F32, U16 = mybir.dt.bfloat16, mybir.dt.float32, mybir.dt.uint16
+SIGMOID = mybir.ActivationFunctionType.Sigmoid
+
+P = 128
+WORDS = 4096
+LEAVES = 1024
+HIDDEN = 512
+BLOCKS = HIDDEN // P
+PER_COLUMN = 16
+
+FLOPS = 2 * 4 * (P * HIDDEN * (LEAVES // 2) + HIDDEN * HIDDEN * (LEAVES // 4) + HIDDEN * HIDDEN * (LEAVES // 8))
+
+
+def tile_treeencoderrnn_b_kernel(
+    tc, table, w_z_l, w_z_r, w_h_l, w_h_r, u_z_l, u_z_r, u_h_l, u_h_r, b_z, b_h, offs, out
+):
+    nc = tc.nc
+    with (
+        tc.tile_pool(name="held", bufs=1) as held,
+        tc.tile_pool(name="work", bufs=BLOCKS) as work,
+        tc.psum_pool(name="psum", bufs=8) as psum,
+    ):
+        offsets = held.tile([P, LEAVES // PER_COLUMN], U16, name="offsets")
+        nc.sync.dma_start(offsets[:], offs)
+        table_sb = held.tile([P, WORDS], BF16, name="table_sb")
+        nc.sync.dma_start(table_sb[:, : WORDS // 2], table[:, : WORDS // 2])
+        nc.scalar.dma_start(table_sb[:, WORDS // 2 :], table[:, WORDS // 2 :])
+
+        def load_w(queue, w, name):
+            w_sb = held.tile([P, HIDDEN], BF16, name=name)
+            queue.dma_start(w_sb[:], w)
+            return w_sb
+
+        def load_bias(queue, b, name):
+            b_sb = held.tile([P, BLOCKS], F32, name=name)
+            with nc.allow_non_contiguous_dma(reason="one float32 bias value to a partition and block"):
+                queue.dma_start(b_sb[:], b.rearrange("(a p) o -> p (a o)", p=P))
+            return b_sb
+
+        def load_u(queue, u, name):
+            u_sb = held.tile([P, BLOCKS, HIDDEN], BF16, name=name)
+            queue.dma_start(u_sb[:], u.rearrange("(k p) m -> p k m", p=P))
+            return u_sb
+
+        w_h = [load_w(nc.sync, w_h_l, "w_h_l_sb"), load_w(nc.scalar, w_h_r, "w_h_r_sb")]
+        bias_h = load_bias(nc.scalar, b_h, "bias_h")
+        w_z = [load_w(nc.sync, w_z_l, "w_z_l_sb"), load_w(nc.scalar, w_z_r, "w_z_r_sb")]
+        bias_z = load_bias(nc.scalar, b_z, "bias_z")
+        u_h = [load_u(nc.sync, u_h_l, "u_h_l_sb"), load_u(nc.scalar, u_h_r, "u_h_r_sb")]
+        u_z = [load_u(nc.sync, u_z_l, "u_z_l_sb"), load_u(nc.scalar, u_z_r, "u_z_r_sb")]
+
+        minus_bias_z = held.tile([P, BLOCKS], F32, name="minus_bias_z")
+        nc.vector.tensor_scalar_mul(minus_bias_z[:], bias_z[:], -1.0)
+
+        def hand_up(state, n, m, level):
+            rounded = held.tile([P, n], BF16, name="rounded_%d_%d" % (level, m))
+            nc.vector.tensor_copy(rounded[:], state[:])
+            pair_sum = held.tile([P, n // 2], F32, name="pair_sum_%d_%d" % (level, m))
+            nc.vector.tensor_add(pair_sum[:], state[:, : n // 2], state[:, n // 2 :])
+            return rounded, pair_sum
+
+        n = LEAVES // 2
+        columns = n // PER_COLUMN
+
+        def project_leaves(w, m):
+            acc = psum.tile([P, n], F32, name="acc", tag="acc")
+            for side in range(2):
+                leaves = table_sb[:].indirect(offsets[:, side * columns : (side + 1) * columns])
+                nc.tensor.matmul(acc[:], w[side][:, m * P : (m + 1) * P], leaves, start=side == 0, stop=side == 1)
+            return acc
+
+        children, child_sums = [], []
+        for m in range(BLOCKS):
+            acc_h = project_leaves(w_h, m)
+            t = work.tile([P, n], F32, name="t")
+            nc.scalar.activation(t[:], acc_h[:], SIGMOID, bias=bias_h[:, m : m + 1])
+            acc_z = project_leaves(w_z, m)
+            one_minus_z = work.tile([P, n], F32, name="one_minus_z")
+            nc.scalar.activation(one_minus_z[:], acc_z[:], SIGMOID, bias=minus_bias_z[:, m : m + 1], scale=-1.0)
+            state = work.tile([P, n], F32, name="state")
+            nc.vector.tensor_mul(state[:], one_minus_z[:], t[:])
+            rounded, pair_sum = hand_up(state, n, m, 1)
+            children.append(rounded)
+            child_sums.append(pair_sum)
+
+        def project_children(acc, u, m, k_blocks, n, children):
+            for k in k_blocks:
+                for side in range(2):
+                    nc.tensor.matmul(
+                        acc[:],
+                        u[side][:, k, m * P : (m + 1) * P],
+                        children[k][:, side * n : (side + 1) * n],
+                        start=k == 0 and side == 0,
+                        stop=k == BLOCKS - 1 and side == 1,
+                    )
+
+        HEAD = 2
+        for level in (2, 3):
+            n = n // 2
+            head = {}
+            for m in range(HEAD):
+                for gate, u in (("h", u_h), ("z", u_z)):
+                    acc = psum.tile([P, n], F32, name="acc", tag="acc")
+                    project_children(acc, u, m, range(BLOCKS - 1), n, children)
+                    head[(m, gate)] = acc
+
+            def gate_sum(gate, u, m):
+                if m < HEAD:
+                    acc = head[(m, gate)]
+                    project_children(acc, u, m, range(BLOCKS - 1, BLOCKS), n, children)
+                else:
+                    acc = psum.tile([P, n], F32, name="acc", tag="acc")
+                    project_children(acc, u, m, range(BLOCKS), n, children)
+                return acc
+
+            parents, parent_sums = [], []
+            for m in range(BLOCKS):
+                acc_h = gate_sum("h", u_h, m)
+                t = work.tile([P, n], F32, name="t")
+                nc.scalar.activation(t[:], acc_h[:], SIGMOID, bias=bias_h[:, m : m + 1])
+                diff = work.tile([P, n], F32, name="diff")
+                nc.vector.tensor_sub(diff[:], child_sums[m][:], t[:])
+                acc_z = gate_sum("z", u_z, m)
+                z = work.tile([P, n], F32, name="z")
+                nc.scalar.activation(z[:], acc_z[:], SIGMOID, bias=bias_z[:, m : m + 1])
+                gated = work.tile([P, n], F32, name="gated")
+                nc.vector.tensor_mul(gated[:], z[:], diff[:])
+                state = work.tile([P, n], F32, name="state")
+                nc.vector.tensor_add(state[:], gated[:], t[:])
+                if level == 2:
+                    rounded, pair_sum = hand_up(state, n, m, level)
+                    parents.append(rounded)
+                    parent_sums.append(pair_sum)
+                else:
+                    nc.sync.dma_start(out[m * P : (m + 1) * P, :], state[:])
+            children, child_sums = parents, parent_sums

@@ -2,6 +2,7 @@ import concourse.mybir as mybir
 
 BF16, F32, U16 = mybir.dt.bfloat16, mybir.dt.float32, mybir.dt.uint16
 SIGMOID = mybir.ActivationFunctionType.Sigmoid
+MULT, ADD = mybir.AluOpType.mult, mybir.AluOpType.add
 
 P = 128
 WORDS = 4096
@@ -9,6 +10,7 @@ LEAVES = 1024
 HIDDEN = 512
 BLOCKS = HIDDEN // P
 PER_COLUMN = 16
+WARM_UP = 8
 
 FLOPS = 2 * 4 * (P * HIDDEN * (LEAVES // 2) + HIDDEN * HIDDEN * (LEAVES // 4) + HIDDEN * HIDDEN * (LEAVES // 8))
 
@@ -54,12 +56,20 @@ def tile_treeencoderrnn_b_kernel(
         minus_bias_z = held.tile([P, BLOCKS], F32, name="minus_bias_z")
         nc.vector.tensor_scalar_mul(minus_bias_z[:], bias_z[:], -1.0)
 
-        def hand_up(state, n, m, level):
+        def hand_up(a, b, op, n, m, level):
             rounded = held.tile([P, n], BF16, name="rounded_%d_%d" % (level, m))
-            nc.vector.tensor_copy(rounded[:], state[:])
+            nc.vector.tensor_tensor(rounded[:], a[:], b[:], op)
+            state = work.tile([P, n], F32, name="state")
+            nc.vector.tensor_tensor(state[:], a[:], b[:], op)
             pair_sum = held.tile([P, n // 2], F32, name="pair_sum_%d_%d" % (level, m))
             nc.vector.tensor_add(pair_sum[:], state[:, : n // 2], state[:, n // 2 :])
             return rounded, pair_sum
+
+        zeros = held.tile([P, HIDDEN], BF16, name="zeros")
+        nc.vector.memset(zeros[:], 0.0)
+        unread = psum.tile([P, HIDDEN], F32, name="acc", tag="acc")
+        for i in range(WARM_UP):
+            nc.tensor.matmul(unread[:], zeros[:, :P], zeros[:], start=True, stop=True)
 
         n = LEAVES // 2
         columns = n // PER_COLUMN
@@ -79,9 +89,7 @@ def tile_treeencoderrnn_b_kernel(
             acc_z = project_leaves(w_z, m)
             one_minus_z = work.tile([P, n], F32, name="one_minus_z")
             nc.scalar.activation(one_minus_z[:], acc_z[:], SIGMOID, bias=minus_bias_z[:, m : m + 1], scale=-1.0)
-            state = work.tile([P, n], F32, name="state")
-            nc.vector.tensor_mul(state[:], one_minus_z[:], t[:])
-            rounded, pair_sum = hand_up(state, n, m, 1)
+            rounded, pair_sum = hand_up(one_minus_z, t, MULT, n, m, 1)
             children.append(rounded)
             child_sums.append(pair_sum)
 
@@ -96,18 +104,19 @@ def tile_treeencoderrnn_b_kernel(
                         stop=k == BLOCKS - 1 and side == 1,
                     )
 
-        HEAD = 2
+        HEAD_BLOCKS = {2: 2, 3: 3}
         for level in (2, 3):
             n = n // 2
+            head_blocks = HEAD_BLOCKS[level]
             head = {}
-            for m in range(HEAD):
+            for m in range(head_blocks):
                 for gate, u in (("h", u_h), ("z", u_z)):
                     acc = psum.tile([P, n], F32, name="acc", tag="acc")
                     project_children(acc, u, m, range(BLOCKS - 1), n, children)
                     head[(m, gate)] = acc
 
             def gate_sum(gate, u, m):
-                if m < HEAD:
+                if m < head_blocks:
                     acc = head[(m, gate)]
                     project_children(acc, u, m, range(BLOCKS - 1, BLOCKS), n, children)
                 else:
@@ -127,12 +136,12 @@ def tile_treeencoderrnn_b_kernel(
                 nc.scalar.activation(z[:], acc_z[:], SIGMOID, bias=bias_z[:, m : m + 1])
                 gated = work.tile([P, n], F32, name="gated")
                 nc.vector.tensor_mul(gated[:], z[:], diff[:])
-                state = work.tile([P, n], F32, name="state")
-                nc.vector.tensor_add(state[:], gated[:], t[:])
                 if level == 2:
-                    rounded, pair_sum = hand_up(state, n, m, level)
+                    rounded, pair_sum = hand_up(gated, t, ADD, n, m, level)
                     parents.append(rounded)
                     parent_sums.append(pair_sum)
                 else:
-                    nc.sync.dma_start(out[m * P : (m + 1) * P, :], state[:])
+                    root = work.tile([P, n], F32, name="root")
+                    nc.vector.tensor_add(root[:], gated[:], t[:])
+                    nc.sync.dma_start(out[m * P : (m + 1) * P, :], root[:])
             children, child_sums = parents, parent_sums

@@ -26,9 +26,12 @@ def tile_treeencoderrnn_b_kernel(
     ):
         offsets = held.tile([P, LEAVES // PER_COLUMN], U16, name="offsets")
         nc.sync.dma_start(offsets[:], offs)
+        w_h_l_sb = held.tile([P, HIDDEN], BF16, name="w_h_l_sb")
+        nc.sync.dma_start(w_h_l_sb[:], w_h_l)
         table_sb = held.tile([P, WORDS], BF16, name="table_sb")
-        nc.sync.dma_start(table_sb[:, : WORDS // 2], table[:, : WORDS // 2])
-        nc.scalar.dma_start(table_sb[:, WORDS // 2 :], table[:, WORDS // 2 :])
+        sync_share = (WORDS - HIDDEN) // 2
+        nc.sync.dma_start(table_sb[:, :sync_share], table[:, :sync_share])
+        nc.scalar.dma_start(table_sb[:, sync_share:], table[:, sync_share:])
 
         def load_w(queue, w, name):
             w_sb = held.tile([P, HIDDEN], BF16, name=name)
@@ -46,7 +49,7 @@ def tile_treeencoderrnn_b_kernel(
             queue.dma_start(u_sb[:], u.rearrange("(k p) m -> p k m", p=P))
             return u_sb
 
-        w_h = [load_w(nc.sync, w_h_l, "w_h_l_sb"), load_w(nc.scalar, w_h_r, "w_h_r_sb")]
+        w_h = [w_h_l_sb, load_w(nc.scalar, w_h_r, "w_h_r_sb")]
         bias_h = load_bias(nc.scalar, b_h, "bias_h")
         w_z = [load_w(nc.sync, w_z_l, "w_z_l_sb"), load_w(nc.scalar, w_z_r, "w_z_r_sb")]
         bias_z = load_bias(nc.scalar, b_z, "bias_z")

@@ -10,7 +10,7 @@ LEAVES = 1024
 HIDDEN = 512
 BLOCKS = HIDDEN // P
 PER_COLUMN = 16
-WARM_UP = 8
+WARM_UP = 4
 
 FLOPS = 2 * 4 * (P * HIDDEN * (LEAVES // 2) + HIDDEN * HIDDEN * (LEAVES // 4) + HIDDEN * HIDDEN * (LEAVES // 8))
 

@@ -27,9 +27,9 @@ def tile_treeencoderrnn_b_kernel(
         offsets = held.tile([P, LEAVES // PER_COLUMN], U16, name="offsets")
         nc.sync.dma_start(offsets[:], offs)
         w_h_l_sb = held.tile([P, HIDDEN], BF16, name="w_h_l_sb")
-        nc.sync.dma_start(w_h_l_sb[:], w_h_l)
+        nc.sync.dma_start(w_h_l_sb[:, :P], w_h_l[:, :P])
         table_sb = held.tile([P, WORDS], BF16, name="table_sb")
-        sync_share = (WORDS - HIDDEN) // 2
+        sync_share = (WORDS - P) // 2
         nc.sync.dma_start(table_sb[:, :sync_share], table[:, :sync_share])
         nc.scalar.dma_start(table_sb[:, sync_share:], table[:, sync_share:])
 
@@ -49,12 +49,13 @@ def tile_treeencoderrnn_b_kernel(
             queue.dma_start(u_sb[:], u.rearrange("(k p) m -> p k m", p=P))
             return u_sb
 
-        w_h = [w_h_l_sb, load_w(nc.scalar, w_h_r, "w_h_r_sb")]
-        bias_h = load_bias(nc.scalar, b_h, "bias_h")
-        w_z = [load_w(nc.sync, w_z_l, "w_z_l_sb"), load_w(nc.scalar, w_z_r, "w_z_r_sb")]
-        bias_z = load_bias(nc.scalar, b_z, "bias_z")
-        u_h = [load_u(nc.sync, u_h_l, "u_h_l_sb"), load_u(nc.scalar, u_h_r, "u_h_r_sb")]
-        u_z = [load_u(nc.sync, u_z_l, "u_z_l_sb"), load_u(nc.scalar, u_z_r, "u_z_r_sb")]
+        w_h = [w_h_l_sb, load_w(nc.sync, w_h_r, "w_h_r_sb")]
+        w_z = [load_w(nc.sync, w_z_l, "w_z_l_sb"), load_w(nc.sync, w_z_r, "w_z_r_sb")]
+        nc.sync.dma_start(w_h_l_sb[:, P:], w_h_l[:, P:])
+        bias_h = load_bias(nc.sync, b_h, "bias_h")
+        bias_z = load_bias(nc.sync, b_z, "bias_z")
+        u_h = [load_u(nc.sync, u_h_l, "u_h_l_sb"), load_u(nc.sync, u_h_r, "u_h_r_sb")]
+        u_z = [load_u(nc.sync, u_z_l, "u_z_l_sb"), load_u(nc.sync, u_z_r, "u_z_r_sb")]
 
         minus_bias_z = held.tile([P, BLOCKS], F32, name="minus_bias_z")
         nc.vector.tensor_scalar_mul(minus_bias_z[:], bias_z[:], -1.0)

@@ -10,7 +10,6 @@ LEAVES = 1024
 HIDDEN = 512
 BLOCKS = HIDDEN // P
 PER_COLUMN = 16
-WARM_UP = 4
 
 FLOPS = 2 * 4 * (P * HIDDEN * (LEAVES // 2) + HIDDEN * HIDDEN * (LEAVES // 4) + HIDDEN * HIDDEN * (LEAVES // 8))
 
@@ -29,9 +28,8 @@ def tile_treeencoderrnn_b_kernel(
         w_h_l_sb = held.tile([P, HIDDEN], BF16, name="w_h_l_sb")
         nc.sync.dma_start(w_h_l_sb[:, :P], w_h_l[:, :P])
         table_sb = held.tile([P, WORDS], BF16, name="table_sb")
-        sync_share = (WORDS - P) // 2
-        nc.sync.dma_start(table_sb[:, :sync_share], table[:, :sync_share])
-        nc.scalar.dma_start(table_sb[:, sync_share:], table[:, sync_share:])
+        nc.sync.dma_start(table_sb[:, : WORDS // 2], table[:, : WORDS // 2])
+        nc.scalar.dma_start(table_sb[:, WORDS // 2 :], table[:, WORDS // 2 :])
 
         def load_w(queue, w, name):
             w_sb = held.tile([P, HIDDEN], BF16, name=name)
@@ -68,12 +66,6 @@ def tile_treeencoderrnn_b_kernel(
             pair_sum = held.tile([P, n // 2], F32, name="pair_sum_%d_%d" % (level, m))
             nc.vector.tensor_add(pair_sum[:], state[:, : n // 2], state[:, n // 2 :])
             return rounded, pair_sum
-
-        zeros = held.tile([P, HIDDEN], BF16, name="zeros")
-        nc.vector.memset(zeros[:], 0.0)
-        unread = psum.tile([P, HIDDEN], F32, name="acc", tag="acc")
-        for i in range(WARM_UP):
-            nc.tensor.matmul(unread[:], zeros[:, :P], zeros[:], start=True, stop=True)
 
         n = LEAVES // 2
         columns = n // PER_COLUMN

@@ -9,6 +9,7 @@ WORDS = 4096
 LEAVES = 1024
 HIDDEN = 512
 BLOCKS = HIDDEN // P
+SYNC_WORDS = 5 * WORDS // 8
 PER_COLUMN = 16
 
 FLOPS = 2 * 4 * (P * HIDDEN * (LEAVES // 2) + HIDDEN * HIDDEN * (LEAVES // 4) + HIDDEN * HIDDEN * (LEAVES // 8))
@@ -28,8 +29,8 @@ def tile_treeencoderrnn_b_kernel(
         w_h_l_sb = held.tile([P, HIDDEN], BF16, name="w_h_l_sb")
         nc.sync.dma_start(w_h_l_sb[:, :P], w_h_l[:, :P])
         table_sb = held.tile([P, WORDS], BF16, name="table_sb")
-        nc.sync.dma_start(table_sb[:, : WORDS // 2], table[:, : WORDS // 2])
-        nc.scalar.dma_start(table_sb[:, WORDS // 2 :], table[:, WORDS // 2 :])
+        nc.sync.dma_start(table_sb[:, :SYNC_WORDS], table[:, :SYNC_WORDS])
+        nc.scalar.dma_start(table_sb[:, SYNC_WORDS:], table[:, SYNC_WORDS:])
 
         def load_w(queue, w, name):
             w_sb = held.tile([P, HIDDEN], BF16, name=name)

@@ -45,14 +45,23 @@ def tile_treeencoderrnn_b_kernel(
 
         def load_u(queue, u, name):
             u_sb = held.tile([P, BLOCKS, HIDDEN], BF16, name=name)
-            queue.dma_start(u_sb[:], u.rearrange("(k p) m -> p k m", p=P))
+            blocks = u.rearrange("(k p) m -> p k m", p=P)
+            half = BLOCKS // 2
+            queue.dma_start(u_sb[:, :half, :], blocks[:, :half, :])
+            queue.dma_start(u_sb[:, half:, :], blocks[:, half:, :])
             return u_sb
 
-        w_h = [w_h_l_sb, load_w(nc.sync, w_h_r, "w_h_r_sb")]
-        w_z = [load_w(nc.sync, w_z_l, "w_z_l_sb"), load_w(nc.sync, w_z_r, "w_z_r_sb")]
-        nc.sync.dma_start(w_h_l_sb[:, P:], w_h_l[:, P:])
+        w_h_r_sb = held.tile([P, HIDDEN], BF16, name="w_h_r_sb")
+        nc.sync.dma_start(w_h_r_sb[:, :P], w_h_r[:, :P])
+        w_z_l_sb = held.tile([P, HIDDEN], BF16, name="w_z_l_sb")
+        nc.sync.dma_start(w_z_l_sb[:, :P], w_z_l[:, :P])
+        w_z_r_sb = load_w(nc.sync, w_z_r, "w_z_r_sb")
         bias_h = load_bias(nc.sync, b_h, "bias_h")
         bias_z = load_bias(nc.sync, b_z, "bias_z")
+        for w_sb, w in ((w_h_l_sb, w_h_l), (w_h_r_sb, w_h_r), (w_z_l_sb, w_z_l)):
+            nc.sync.dma_start(w_sb[:, P:], w[:, P:])
+        w_h = [w_h_l_sb, w_h_r_sb]
+        w_z = [w_z_l_sb, w_z_r_sb]
         u_h = [load_u(nc.sync, u_h_l, "u_h_l_sb"), load_u(nc.sync, u_h_r, "u_h_r_sb")]
         u_z = [load_u(nc.sync, u_z_l, "u_z_l_sb"), load_u(nc.sync, u_z_r, "u_z_r_sb")]
 

import concourse.mybir as mybir

BF16, F32, U16 = mybir.dt.bfloat16, mybir.dt.float32, mybir.dt.uint16
SIGMOID = mybir.ActivationFunctionType.Sigmoid
MULT, ADD = mybir.AluOpType.mult, mybir.AluOpType.add

P = 128
WORDS = 4096
LEAVES = 1024
HIDDEN = 512
BLOCKS = HIDDEN // P
SYNC_WORDS = 5 * WORDS // 8
PER_COLUMN = 16

FLOPS = 2 * 4 * (P * HIDDEN * (LEAVES // 2) + HIDDEN * HIDDEN * (LEAVES // 4) + HIDDEN * HIDDEN * (LEAVES // 8))


def tile_treeencoderrnn_b_kernel(
    tc, table, w_z_l, w_z_r, w_h_l, w_h_r, u_z_l, u_z_r, u_h_l, u_h_r, b_z, b_h, offs, out
):
    nc = tc.nc
    with (
        tc.tile_pool(name="held", bufs=1) as held,
        tc.tile_pool(name="work", bufs=BLOCKS) as work,
        tc.psum_pool(name="psum", bufs=8) as psum,
    ):
        offsets = held.tile([P, LEAVES // PER_COLUMN], U16, name="offsets")
        nc.sync.dma_start(offsets[:], offs)
        w_h_l_sb = held.tile([P, HIDDEN], BF16, name="w_h_l_sb")
        nc.sync.dma_start(w_h_l_sb[:, :P], w_h_l[:, :P])
        table_sb = held.tile([P, WORDS], BF16, name="table_sb")
        nc.sync.dma_start(table_sb[:, :SYNC_WORDS], table[:, :SYNC_WORDS])
        nc.scalar.dma_start(table_sb[:, SYNC_WORDS:], table[:, SYNC_WORDS:])

        def load_w(queue, w, name):
            w_sb = held.tile([P, HIDDEN], BF16, name=name)
            queue.dma_start(w_sb[:], w)
            return w_sb

        def load_bias(queue, b, name):
            b_sb = held.tile([P, BLOCKS], F32, name=name)
            with nc.allow_non_contiguous_dma(reason="one float32 bias value to a partition and block"):
                queue.dma_start(b_sb[:], b.rearrange("(a p) o -> p (a o)", p=P))
            return b_sb

        def load_u(queue, u, name):
            u_sb = held.tile([P, BLOCKS, HIDDEN], BF16, name=name)
            blocks = u.rearrange("(k p) m -> p k m", p=P)
            half = BLOCKS // 2
            queue.dma_start(u_sb[:, :half, :], blocks[:, :half, :])
            queue.dma_start(u_sb[:, half:, :], blocks[:, half:, :])
            return u_sb

        w_h_r_sb = held.tile([P, HIDDEN], BF16, name="w_h_r_sb")
        nc.sync.dma_start(w_h_r_sb[:, :P], w_h_r[:, :P])
        w_z_l_sb = held.tile([P, HIDDEN], BF16, name="w_z_l_sb")
        nc.sync.dma_start(w_z_l_sb[:, :P], w_z_l[:, :P])
        w_z_r_sb = load_w(nc.sync, w_z_r, "w_z_r_sb")
        bias_h = load_bias(nc.sync, b_h, "bias_h")
        bias_z = load_bias(nc.sync, b_z, "bias_z")
        for w_sb, w in ((w_h_l_sb, w_h_l), (w_h_r_sb, w_h_r), (w_z_l_sb, w_z_l)):
            nc.sync.dma_start(w_sb[:, P:], w[:, P:])
        w_h = [w_h_l_sb, w_h_r_sb]
        w_z = [w_z_l_sb, w_z_r_sb]
        u_h = [load_u(nc.sync, u_h_l, "u_h_l_sb"), load_u(nc.sync, u_h_r, "u_h_r_sb")]
        u_z = [load_u(nc.sync, u_z_l, "u_z_l_sb"), load_u(nc.sync, u_z_r, "u_z_r_sb")]

        minus_bias_z = held.tile([P, BLOCKS], F32, name="minus_bias_z")
        nc.vector.tensor_scalar_mul(minus_bias_z[:], bias_z[:], -1.0)

        def hand_up(a, b, op, n, m, level):
            rounded = held.tile([P, n], BF16, name="rounded_%d_%d" % (level, m))
            nc.vector.tensor_tensor(rounded[:], a[:], b[:], op)
            state = work.tile([P, n], F32, name="state")
            nc.vector.tensor_tensor(state[:], a[:], b[:], op)
            pair_sum = held.tile([P, n // 2], F32, name="pair_sum_%d_%d" % (level, m))
            nc.vector.tensor_add(pair_sum[:], state[:, : n // 2], state[:, n // 2 :])
            return rounded, pair_sum

        n = LEAVES // 2
        columns = n // PER_COLUMN

        def project_leaves(w, m):
            acc = psum.tile([P, n], F32, name="acc", tag="acc")
            for side in range(2):
                leaves = table_sb[:].indirect(offsets[:, side * columns : (side + 1) * columns])
                nc.tensor.matmul(acc[:], w[side][:, m * P : (m + 1) * P], leaves, start=side == 0, stop=side == 1)
            return acc

        children, child_sums = [], []
        for m in range(BLOCKS):
            acc_h = project_leaves(w_h, m)
            t = work.tile([P, n], F32, name="t")
            nc.scalar.activation(t[:], acc_h[:], SIGMOID, bias=bias_h[:, m : m + 1])
            acc_z = project_leaves(w_z, m)
            one_minus_z = work.tile([P, n], F32, name="one_minus_z")
            nc.scalar.activation(one_minus_z[:], acc_z[:], SIGMOID, bias=minus_bias_z[:, m : m + 1], scale=-1.0)
            rounded, pair_sum = hand_up(one_minus_z, t, MULT, n, m, 1)
            children.append(rounded)
            child_sums.append(pair_sum)

        def project_children(acc, u, m, k_blocks, n, children):
            for k in k_blocks:
                for side in range(2):
                    nc.tensor.matmul(
                        acc[:],
                        u[side][:, k, m * P : (m + 1) * P],
                        children[k][:, side * n : (side + 1) * n],
                        start=k == 0 and side == 0,
                        stop=k == BLOCKS - 1 and side == 1,
                    )

        HEAD_BLOCKS = {2: 2, 3: 3}
        for level in (2, 3):
            n = n // 2
            head_blocks = HEAD_BLOCKS[level]
            head = {}
            for m in range(head_blocks):
                for gate, u in (("h", u_h), ("z", u_z)):
                    acc = psum.tile([P, n], F32, name="acc", tag="acc")
                    project_children(acc, u, m, range(BLOCKS - 1), n, children)
                    head[(m, gate)] = acc

            def gate_sum(gate, u, m):
                if m < head_blocks:
                    acc = head[(m, gate)]
                    project_children(acc, u, m, range(BLOCKS - 1, BLOCKS), n, children)
                else:
                    acc = psum.tile([P, n], F32, name="acc", tag="acc")
                    project_children(acc, u, m, range(BLOCKS), n, children)
                return acc

            parents, parent_sums = [], []
            for m in range(BLOCKS):
                acc_h = gate_sum("h", u_h, m)
                t = work.tile([P, n], F32, name="t")
                nc.scalar.activation(t[:], acc_h[:], SIGMOID, bias=bias_h[:, m : m + 1])
                diff = work.tile([P, n], F32, name="diff")
                nc.vector.tensor_sub(diff[:], child_sums[m][:], t[:])
                acc_z = gate_sum("z", u_z, m)
                z = work.tile([P, n], F32, name="z")
                nc.scalar.activation(z[:], acc_z[:], SIGMOID, bias=bias_z[:, m : m + 1])
                gated = work.tile([P, n], F32, name="gated")
                nc.vector.tensor_mul(gated[:], z[:], diff[:])
                if level == 2:
                    rounded, pair_sum = hand_up(gated, t, ADD, n, m, level)
                    parents.append(rounded)
                    parent_sums.append(pair_sum)
                else:
                    root = work.tile([P, n], F32, name="root")
                    nc.vector.tensor_add(root[:], gated[:], t[:])
                    nc.sync.dma_start(out[m * P : (m + 1) * P, :], root[:])
            children, child_sums = parents, parent_sums
